import numpy as np
import ml_dtypes


def mxq(x, axis, fmt="e4m3"):
    dtype, down = {"e4m3": (ml_dtypes.float8_e4m3fn, 7), "e5m2": (ml_dtypes.float8_e5m2, 14)}[fmt]
    v = np.moveaxis(np.asarray(x, np.float32).astype(ml_dtypes.bfloat16).astype(np.float64), axis, -1)
    blocks = v.reshape(v.shape[:-1] + (-1, 32))
    amax = np.abs(blocks).max(-1, keepdims=True)
    byte = np.maximum(np.where(amax > 0, np.frexp(amax)[1] - 1 + 127, 0) - down, 1)
    scale = np.exp2(byte - 127.0)
    codes = (blocks / scale).astype(np.float32).astype(dtype).astype(np.float64)
    return np.moveaxis((codes * scale).reshape(v.shape), -1, axis)


WIDE = False


def mx_kscale(k):
    if not WIDE:
        return np.ones(k)
    levels = np.array([10, -10, 5, -5, 0])
    if k % 512:
        return np.exp2(np.random.permutation(np.resize(levels, k // 32))).repeat(32)
    a = np.empty((k // 512, 16))
    for p in range(k // 512):
        a[p, :8] = np.random.permutation(np.resize(levels, 8))
        for g in range(8):
            far = levels[np.abs(levels - a[p, g]) >= 10]
            a[p, g + 8] = far[np.random.randint(len(far))]
    return np.exp2(a.ravel()).repeat(32)


BF16 = ml_dtypes.bfloat16


def bf(x):
    return np.asarray(x, np.float32).astype(BF16)


def f64(x):
    return np.asarray(x).astype(np.float64)


B, S, D, H, QL, KL, ND, VD, RD = 4, 1024, 1024, 4, 512, 512, 64, 64, 128
BASE = 10000.0


def rope(v):
    d = v.shape[-1]
    inv_freq = BASE ** (-np.arange(0, d, 2) / d)
    ang = np.arange(v.shape[1])[:, None] * inv_freq[None, :]
    cos = np.cos(ang)[None, :, None, :]
    sin = np.sin(ang)[None, :, None, :]
    v1 = v[..., 0::2]
    v2 = v[..., 1::2]
    o1 = v1 * cos - v2 * sin
    o2 = v1 * sin + v2 * cos
    return np.stack([o1, o2], axis=-1).reshape(v.shape)


def setup_inputs():
    s, t = mx_kscale(D), mx_kscale(KL)
    tc = np.concatenate([t, np.ones(RD)])
    return {"x": bf(np.random.standard_normal((B, S, D)) * s),
            "Wkva": bf(np.random.standard_normal((D, KL + RD)) / np.sqrt(D) / s[:, None] * tc),
            "Wkvb": bf(np.random.standard_normal((KL, H * (ND + VD))) / np.sqrt(KL) / t[:, None])}


def reference(x, Wkva, Wkvb):
    ckv = mxq(f64(x), 2, "e4m3") @ mxq(f64(Wkva), 0, "e4m3")
    compressed_kv, k_pe = ckv[..., :KL], ckv[..., KL:]
    k_pe = np.broadcast_to(k_pe[:, :, None, :], (B, S, H, RD))
    kv = (mxq(compressed_kv, 2, "e4m3") @ mxq(f64(Wkvb), 0, "e4m3")).reshape(B, S, H, ND + VD)
    k_nope, v = kv[..., :ND], kv[..., ND:]
    kf = np.concatenate([k_nope, rope(k_pe)], axis=-1)
    return kf, v

@@ -1,0 +1,336 @@
+import math
+from contextlib import ExitStack
+
+import concourse.mybir as mybir
+from concourse.masks import make_identity
+
+F32 = mybir.dt.float32
+BF16 = mybir.dt.bfloat16
+I32 = mybir.dt.int32
+U32 = mybir.dt.uint32
+U8 = mybir.dt.uint8
+FP8X4 = mybir.dt.float8_e4m3fn_x4
+ALU = mybir.AluOpType
+ACT = mybir.ActivationFunctionType
+
+P = 128
+PACK = 4
+TOKENS = 4 * 1024
+SEQ = 1024
+D = 1024
+PASSES = D // (P * PACK)
+KL = 512
+RD = 128
+PAIRS = RD // 2
+H = 4
+ND = 64
+VD = 64
+CKV = KL + RD
+KV = H * (ND + VD)
+ROPE_BASE = 10000.0
+
+TILES = 2
+UNIT = TILES * P
+UNITS = TOKENS // UNIT
+PHASES = SEQ // UNIT
+
+ROUND_MAGIC = 1.5 * 2.0**23
+
+FLOPS = 2 * TOKENS * D * CKV + 2 * TOKENS * KL * KV
+
+
+def tile_multilatentattention_pb_t_kernel(tc, x, Wkva, Wkvb, out_0, out_1):
+    nc = tc.nc
+    x_units = x.flatten_outer_dims().rearrange("(n p i) k -> n p (i k)", p=P, i=TILES)
+    kf_units = out_0.rearrange("b s h f -> (b s) (h f)").rearrange(
+        "(n p i) f -> n p (i f)", p=P, i=TILES
+    )
+    v_units = out_1.rearrange("b s h f -> (b s) (h f)").rearrange(
+        "(n p i) f -> n p (i f)", p=P, i=TILES
+    )
+
+    with ExitStack() as ctx:
+        keep = ctx.enter_context(tc.tile_pool(name="keep", bufs=1))
+        x_pool = ctx.enter_context(tc.tile_pool(name="x_pool", bufs=UNITS))
+        stage = ctx.enter_context(tc.tile_pool(name="stage", bufs=3))
+        codes = ctx.enter_context(tc.tile_pool(name="codes", bufs=3))
+        results = ctx.enter_context(tc.tile_pool(name="results", bufs=8))
+        xt_banks = ctx.enter_context(tc.psum_pool(name="xt_banks", bufs=3))
+        c_banks = ctx.enter_context(tc.psum_pool(name="c_banks", bufs=2))
+        kv_banks = ctx.enter_context(tc.psum_pool(name="kv_banks", bufs=2))
+        pe_banks = ctx.enter_context(tc.psum_pool(name="pe_banks", bufs=1))
+        ctx.enter_context(tc.manual_schedule())
+
+        wa_rows = Wkva.rearrange("(g q t) c -> g q (t c)", g=PASSES, q=P, t=PACK)
+        wa_raw = keep.tile([P, PASSES, PACK, CKV], BF16)
+        for g in range(PASSES):
+            nc.sync.dma_start(out=wa_raw[:, g].rearrange("q t c -> q (t c)"), in_=wa_rows[g])
+        x_sb = {}
+
+        def load_x(n):
+            x_sb[n] = x_pool.tile([P, TILES * D], BF16, name="x_sb")
+            nc.sync.dma_start(out=x_sb[n][:], in_=x_units[n])
+
+        load_x(0)
+        load_x(1)
+        wb_raw = keep.tile([P, PACK, KV], BF16)
+        nc.sync.dma_start(out=wb_raw[:], in_=Wkvb.rearrange("(q m) n -> q m n", q=P))
+        for n in range(2, UNITS):
+            load_x(n)
+
+        warm = keep.tile([P, 1], F32)
+        nc.vector.memset(warm[:], 0.0)
+        nc.scalar.activation(out=warm[:], in_=warm[:], func=ACT.Sin)
+        pos_i = keep.tile([P, PHASES * TILES], I32)
+        nc.gpsimd.iota(
+            pos_i[:], pattern=[[UNIT, PHASES], [1, TILES]], base=0, channel_multiplier=TILES
+        )
+        ident = keep.tile([P, P], F32)
+        make_identity(nc, ident[:])
+        pos = keep.tile([P, PHASES * TILES], F32)
+        nc.vector.tensor_copy(out=pos[:], in_=pos_i[:])
+        turns = keep.tile([P, PAIRS], F32)
+        nc.vector.memset(turns[:, 0:1], 1.0)
+        nc.vector.tensor_scalar_mul(out=turns[:, 0:1], in0=turns[:, 0:1], scalar1=0.5 / math.pi)
+        filled = 1
+        while filled < PAIRS:
+            nc.vector.tensor_scalar_mul(
+                out=turns[:, filled : 2 * filled],
+                in0=turns[:, 0:filled],
+                scalar1=ROPE_BASE ** (-2.0 * filled / RD),
+            )
+            filled *= 2
+        table_shape = [P, PHASES * TILES, PAIRS]
+        angle = keep.tile(table_shape, F32)
+        nc.vector.tensor_tensor(
+            out=angle[:],
+            in0=pos[:].unsqueeze(2).to_broadcast(table_shape),
+            in1=turns[:].unsqueeze(1).to_broadcast(table_shape),
+            op=ALU.mult,
+        )
+        whole = keep.tile(table_shape, F32)
+        nc.vector.tensor_scalar(
+            out=whole[:],
+            in0=angle[:],
+            scalar1=ROUND_MAGIC,
+            scalar2=ROUND_MAGIC,
+            op0=ALU.add,
+            op1=ALU.subtract,
+        )
+        frac = keep.tile(table_shape, F32)
+        nc.vector.tensor_sub(out=frac[:], in0=angle[:], in1=whole[:])
+        sin_t = keep.tile(table_shape, F32)
+        sin_half = keep.tile(table_shape, F32)
+        cos_t = keep.tile(table_shape, F32)
+        nc.scalar.activation(out=sin_t[:], in_=frac[:], func=ACT.Sin, scale=2.0 * math.pi)
+        nc.scalar.activation(out=sin_half[:], in_=frac[:], func=ACT.Sin, scale=math.pi)
+        nc.scalar.activation(out=sin_half[:], in_=sin_half[:], func=ACT.Square)
+        nc.scalar.activation(out=cos_t[:], in_=sin_half[:], func=ACT.Copy, scale=-2.0, bias=1.0)
+
+        def regroup(engine_copy, grouped, raw):
+            engine_copy(
+                out=grouped.rearrange("q (c r) t -> q c t r", r=4),
+                in_=raw.rearrange("q t (c r) -> q c t r", r=4),
+            )
+
+        def quantise(words, scales, grouped):
+            nc.vector.quantize_mx(
+                out=words.bitcast(FP8X4), scales=scales, in_=grouped.rearrange("q c t -> q (c t)")
+            )
+
+        wa_grouped = keep.tile([P, PASSES, CKV, PACK], BF16, align_bytes=64)
+        wa_codes = keep.tile([P, PASSES, CKV], U32, align_bytes=64)
+        wa_scales = keep.tile([P, PASSES, CKV], U8, align_bytes=64)
+        latent_cols = slice(0, KL)
+        rope_cols = slice(KL, CKV)
+        for g in range(PASSES):
+            nc.vector.tensor_copy(
+                out=wa_grouped[:, g, latent_cols, :].rearrange("q (m j) t -> q m j t", m=PACK),
+                in_=wa_raw[:, g, :, latent_cols].rearrange("q t (j m) -> q m j t", m=PACK),
+            )
+            nc.scalar.copy(
+                out=wa_grouped[:, g, rope_cols, :].rearrange("q (e j) t -> q e j t", e=2),
+                in_=wa_raw[:, g, :, rope_cols].rearrange("q t (j e) -> q e j t", e=2),
+            )
+            quantise(
+                wa_codes[:, g, latent_cols], wa_scales[:, g, latent_cols], wa_grouped[:, g, latent_cols, :]
+            )
+        wb_grouped = keep.tile([P, KV, PACK], BF16, align_bytes=64)
+        wb_codes = keep.tile([P, KV], U32, align_bytes=64)
+        wb_scales = keep.tile([P, KV], U8, align_bytes=64)
+
+        x_grouped = {}
+        x_codes = {}
+        x_scales = {}
+        c_grouped = {}
+        c_codes = {}
+        c_scales = {}
+        rope_a = {}
+        rope_b = {}
+        kf_t = {}
+        v_t = {}
+        half = D // 2
+
+        def transpose_unit(n):
+            x_grouped[n] = stage.tile([P, TILES * D], BF16, name="x_grouped", align_bytes=64)
+            words_in = x_sb[n][:].bitcast(F32)
+            words_out = x_grouped[n][:].bitcast(F32)
+            for i in range(TILES):
+                xt = xt_banks.tile([P, half], F32, name="xt")
+                for g in range(PASSES):
+                    first = i * half + g * 2 * P
+                    for u in range(2):
+                        nc.tensor.transpose(
+                            xt[:, (2 * g + u) * P : (2 * g + u + 1) * P],
+                            words_in[:, first + u : first + 2 * P : 2],
+                            ident[:],
+                        )
+                nc.scalar.copy(
+                    out=words_out[:, i * half : (i + 1) * half].rearrange(
+                        "q (g r u) -> q g r u", g=PASSES, u=2
+                    ),
+                    in_=xt[:].rearrange("q (g u r) -> q g r u", g=PASSES, u=2),
+                )
+
+        def quantise_x(n):
+            x_codes[n] = codes.tile([P, TILES * PASSES * P], U32, name="x_codes", align_bytes=64)
+            x_scales[n] = codes.tile([P, TILES * PASSES * P], U8, name="x_scales", align_bytes=64)
+            for i in range(TILES):
+                cols = slice(i * PASSES * P, (i + 1) * PASSES * P)
+                nc.vector.quantize_mx(
+                    out=x_codes[n][:, cols].bitcast(FP8X4),
+                    scales=x_scales[n][:, cols],
+                    in_=x_grouped[n][:, i * D : (i + 1) * D],
+                )
+
+        def x_cols(i, g):
+            return slice((i * PASSES + g) * P, (i * PASSES + g + 1) * P)
+
+        def rope_products(n):
+            pe = pe_banks.tile([P, TILES, 2, PAIRS], F32, name="pe")
+            for i in range(TILES):
+                for g in range(PASSES):
+                    nc.tensor.matmul_mx(
+                        out=pe[:, i].rearrange("p e j -> p (e j)"),
+                        lhsT=x_codes[n][:, x_cols(i, g)].bitcast(FP8X4),
+                        lhsT_scale=x_scales[n][:, x_cols(i, g)],
+                        rhs=wa_codes[:, g, rope_cols].bitcast(FP8X4),
+                        rhs_scale=wa_scales[:, g, rope_cols],
+                        start=(g == 0),
+                        stop=(g == PASSES - 1),
+                    )
+            ph = n % PHASES
+            rows = slice(ph * TILES, (ph + 1) * TILES)
+            rope_a[n] = stage.tile([P, TILES, 2, PAIRS], F32, name="rope_a")
+            rope_b[n] = stage.tile([P, TILES, 2, PAIRS], F32, name="rope_b")
+            nc.vector.tensor_tensor(
+                out=rope_a[n][:],
+                in0=pe[:],
+                in1=cos_t[:, rows, :].unsqueeze(2).to_broadcast([P, TILES, 2, PAIRS]),
+                op=ALU.mult,
+            )
+            nc.vector.scalar_tensor_tensor(
+                out=rope_b[n][:, :, 0, :],
+                in0=pe[:, :, 1, :],
+                scalar=-1.0,
+                in1=sin_t[:, rows, :],
+                op0=ALU.mult,
+                op1=ALU.mult,
+            )
+            nc.vector.tensor_tensor(
+                out=rope_b[n][:, :, 1, :], in0=pe[:, :, 0, :], in1=sin_t[:, rows, :], op=ALU.mult
+            )
+
+        def rope_finish(n):
+            kf_t[n] = results.tile([P, TILES, H, ND + RD], F32, name="kf_t")
+            nc.vector.tensor_tensor(
+                out=kf_t[n][:, :, 0, ND:].rearrange("p i (j e) -> p i j e", e=2),
+                in0=rope_a[n][:].rearrange("p i e j -> p i j e"),
+                in1=rope_b[n][:].rearrange("p i e j -> p i j e"),
+                op=ALU.add,
+            )
+            nc.gpsimd.tensor_scalar(
+                out=kf_t[n][:, :, 1:H, ND:],
+                in0=kf_t[n][:, :, 0:1, ND:].to_broadcast([P, TILES, H - 1, RD]),
+                scalar1=1.0,
+                scalar2=0.0,
+                op0=ALU.mult,
+                op1=ALU.add,
+            )
+
+        def latent(n, i):
+            cb = c_banks.tile([P, PACK, P], F32, name="cb")
+            for m in range(PACK):
+                for g in range(PASSES):
+                    nc.tensor.matmul_mx(
+                        out=cb[:, m, :],
+                        lhsT=wa_codes[:, g, m * P : (m + 1) * P].bitcast(FP8X4),
+                        lhsT_scale=wa_scales[:, g, m * P : (m + 1) * P],
+                        rhs=x_codes[n][:, x_cols(i, g)].bitcast(FP8X4),
+                        rhs_scale=x_scales[n][:, x_cols(i, g)],
+                        start=(g == 0),
+                        stop=(g == PASSES - 1),
+                    )
+            c_grouped[n, i] = stage.tile([P, P, PACK], BF16, name="c_grouped%d" % i, align_bytes=64)
+            if i == 0:
+                nc.vector.tensor_copy(out=c_grouped[n, i][:], in_=cb[:].rearrange("q m r -> q r m"))
+            else:
+                nc.scalar.copy(out=c_grouped[n, i][:], in_=cb[:].rearrange("q m r -> q r m"))
+
+        def quantise_latent(n, i):
+            c_codes[n, i] = codes.tile([P, P], U32, name="c_codes%d" % i, align_bytes=64)
+            c_scales[n, i] = codes.tile([P, P], U8, name="c_scales%d" % i, align_bytes=64)
+            quantise(c_codes[n, i][:], c_scales[n, i][:], c_grouped[n, i][:])
+
+        def expand(n, i):
+            kv = kv_banks.tile([P, H, 2, ND], F32, name="kv")
+            nc.tensor.matmul_mx(
+                out=kv[:].rearrange("p h s d -> p (h s d)"),
+                lhsT=c_codes[n, i][:].bitcast(FP8X4),
+                lhsT_scale=c_scales[n, i][:],
+                rhs=wb_codes[:].bitcast(FP8X4),
+                rhs_scale=wb_scales[:],
+                start=True,
+                stop=True,
+            )
+            if i == 0:
+                v_t[n] = results.tile([P, TILES, H, VD], F32, name="v_t")
+            nc.scalar.copy(out=kf_t[n][:, i, :, 0:ND], in_=kv[:, :, 0, :])
+            nc.scalar.copy(out=v_t[n][:, i, :, :], in_=kv[:, :, 1, :])
+
+        def store(n):
+            nc.sync.dma_start(out=kf_units[n], in_=kf_t[n][:].rearrange("p i h f -> p (i h f)"))
+            nc.sync.dma_start(out=v_units[n], in_=v_t[n][:].rearrange("p i h f -> p (i h f)"))
+
+        def live(n):
+            return 0 <= n < UNITS
+
+        def turn(n):
+            if live(n):
+                latent(n, 0)
+                latent(n, 1)
+            if live(n + 1):
+                quantise_x(n + 1)
+            if live(n):
+                quantise_latent(n, 0)
+                rope_products(n)
+                quantise_latent(n, 1)
+            if live(n - 1):
+                expand(n - 1, 0)
+                expand(n - 1, 1)
+                store(n - 1)
+            if live(n + 2):
+                transpose_unit(n + 2)
+            if live(n):
+                rope_finish(n)
+
+        turn(-2)
+        turn(-1)
+        for g in range(PASSES):
+            quantise(wa_codes[:, g, rope_cols], wa_scales[:, g, rope_cols], wa_grouped[:, g, rope_cols, :])
+        regroup(nc.vector.tensor_copy, wb_grouped[:, 0 : KV // 2, :], wb_raw[:, :, 0 : KV // 2])
+        regroup(nc.scalar.copy, wb_grouped[:, KV // 2 : KV, :], wb_raw[:, :, KV // 2 : KV])
+        turn(0)
+        quantise(wb_codes[:], wb_scales[:], wb_grouped[:])
+        for n in range(1, UNITS + 1):
+            turn(n)

@@ -119,13 +119,19 @@ def tile_multilatentattention_pb_t_kernel(tc, x, Wkva, Wkvb, out_0, out_1):
         )
         frac = keep.tile(table_shape, F32)
         nc.vector.tensor_sub(out=frac[:], in0=angle[:], in1=whole[:])
-        sin_t = keep.tile(table_shape, F32)
         sin_half = keep.tile(table_shape, F32)
-        cos_t = keep.tile(table_shape, F32)
-        nc.scalar.activation(out=sin_t[:], in_=frac[:], func=ACT.Sin, scale=2.0 * math.pi)
+        factors = keep.tile([P, PHASES * TILES, 2, 2, PAIRS], F32)
+        nc.scalar.activation(out=factors[:, :, 1, 0, :], in_=frac[:], func=ACT.Sin, scale=2.0 * math.pi)
+        nc.scalar.activation(out=factors[:, :, 1, 1, :], in_=frac[:], func=ACT.Sin, scale=-2.0 * math.pi)
         nc.scalar.activation(out=sin_half[:], in_=frac[:], func=ACT.Sin, scale=math.pi)
         nc.scalar.activation(out=sin_half[:], in_=sin_half[:], func=ACT.Square)
-        nc.scalar.activation(out=cos_t[:], in_=sin_half[:], func=ACT.Copy, scale=-2.0, bias=1.0)
+        nc.scalar.activation(
+            out=factors[:, :, 0, :, :],
+            in_=sin_half[:].unsqueeze(2).to_broadcast([P, PHASES * TILES, 2, PAIRS]),
+            func=ACT.Copy,
+            scale=-2.0,
+            bias=1.0,
+        )
 
         def regroup(engine_copy, grouped, raw):
             engine_copy(
@@ -165,8 +171,7 @@ def tile_multilatentattention_pb_t_kernel(tc, x, Wkva, Wkvb, out_0, out_1):
         c_grouped = {}
         c_codes = {}
         c_scales = {}
-        rope_a = {}
-        rope_b = {}
+        products = {}
         kf_t = {}
         v_t = {}
         half = D // 2
@@ -195,13 +200,9 @@ def tile_multilatentattention_pb_t_kernel(tc, x, Wkva, Wkvb, out_0, out_1):
         def quantise_x(n):
             x_codes[n] = codes.tile([P, TILES * PASSES * P], U32, name="x_codes", align_bytes=64)
             x_scales[n] = codes.tile([P, TILES * PASSES * P], U8, name="x_scales", align_bytes=64)
-            for i in range(TILES):
-                cols = slice(i * PASSES * P, (i + 1) * PASSES * P)
-                nc.vector.quantize_mx(
-                    out=x_codes[n][:, cols].bitcast(FP8X4),
-                    scales=x_scales[n][:, cols],
-                    in_=x_grouped[n][:, i * D : (i + 1) * D],
-                )
+            nc.vector.quantize_mx(
+                out=x_codes[n][:].bitcast(FP8X4), scales=x_scales[n][:], in_=x_grouped[n][:]
+            )
 
         def x_cols(i, g):
             return slice((i * PASSES + g) * P, (i * PASSES + g + 1) * P)
@@ -219,34 +220,25 @@ def tile_multilatentattention_pb_t_kernel(tc, x, Wkva, Wkvb, out_0, out_1):
                         start=(g == 0),
                         stop=(g == PASSES - 1),
                     )
-            ph = n % PHASES
-            rows = slice(ph * TILES, (ph + 1) * TILES)
-            rope_a[n] = stage.tile([P, TILES, 2, PAIRS], F32, name="rope_a")
-            rope_b[n] = stage.tile([P, TILES, 2, PAIRS], F32, name="rope_b")
+            row = (n % PHASES) * TILES
+            products[n] = stage.tile([P, 2, TILES, 2 * PAIRS], F32, name="products")
             nc.vector.tensor_tensor(
-                out=rope_a[n][:],
-                in0=pe[:],
-                in1=cos_t[:, rows, :].unsqueeze(2).to_broadcast([P, TILES, 2, PAIRS]),
+                out=products[n][:],
+                in0=pe[:]
+                .rearrange("p i e j -> p i (e j)")
+                .unsqueeze(1)
+                .to_broadcast([P, 2, TILES, 2 * PAIRS]),
+                in1=factors[:, row : row + TILES].rearrange("p i k e j -> p k i (e j)"),
                 op=ALU.mult,
-            )
-            nc.vector.scalar_tensor_tensor(
-                out=rope_b[n][:, :, 0, :],
-                in0=pe[:, :, 1, :],
-                scalar=-1.0,
-                in1=sin_t[:, rows, :],
-                op0=ALU.mult,
-                op1=ALU.mult,
-            )
-            nc.vector.tensor_tensor(
-                out=rope_b[n][:, :, 1, :], in0=pe[:, :, 0, :], in1=sin_t[:, rows, :], op=ALU.mult
             )
 
         def rope_finish(n):
             kf_t[n] = results.tile([P, TILES, H, ND + RD], F32, name="kf_t")
+            halves = products[n][:].rearrange("p k i (e j) -> p k i j e", e=2)
             nc.vector.tensor_tensor(
                 out=kf_t[n][:, :, 0, ND:].rearrange("p i (j e) -> p i j e", e=2),
-                in0=rope_a[n][:].rearrange("p i e j -> p i j e"),
-                in1=rope_b[n][:].rearrange("p i e j -> p i j e"),
+                in0=halves[:, 0],
+                in1=halves[:, 1, :, :, ::-1],
                 op=ALU.add,
             )
             nc.gpsimd.tensor_scalar(
@@ -271,23 +263,28 @@ def tile_multilatentattention_pb_t_kernel(tc, x, Wkva, Wkvb, out_0, out_1):
                         start=(g == 0),
                         stop=(g == PASSES - 1),
                     )
-            c_grouped[n, i] = stage.tile([P, P, PACK], BF16, name="c_grouped%d" % i, align_bytes=64)
             if i == 0:
-                nc.vector.tensor_copy(out=c_grouped[n, i][:], in_=cb[:].rearrange("q m r -> q r m"))
+                c_grouped[n] = stage.tile([P, TILES, P, PACK], BF16, name="c_grouped", align_bytes=64)
+            if i == 0:
+                nc.vector.tensor_copy(out=c_grouped[n][:, i], in_=cb[:].rearrange("q m r -> q r m"))
             else:
-                nc.scalar.copy(out=c_grouped[n, i][:], in_=cb[:].rearrange("q m r -> q r m"))
+                nc.scalar.copy(out=c_grouped[n][:, i], in_=cb[:].rearrange("q m r -> q r m"))
 
-        def quantise_latent(n, i):
-            c_codes[n, i] = codes.tile([P, P], U32, name="c_codes%d" % i, align_bytes=64)
-            c_scales[n, i] = codes.tile([P, P], U8, name="c_scales%d" % i, align_bytes=64)
-            quantise(c_codes[n, i][:], c_scales[n, i][:], c_grouped[n, i][:])
+        def quantise_latent(n):
+            c_codes[n] = codes.tile([P, TILES, P], U32, name="c_codes", align_bytes=64)
+            c_scales[n] = codes.tile([P, TILES, P], U8, name="c_scales", align_bytes=64)
+            nc.vector.quantize_mx(
+                out=c_codes[n][:].rearrange("q i r -> q (i r)").bitcast(FP8X4),
+                scales=c_scales[n][:].rearrange("q i r -> q (i r)"),
+                in_=c_grouped[n][:].rearrange("q i r t -> q (i r t)"),
+            )
 
         def expand(n, i):
             kv = kv_banks.tile([P, H, 2, ND], F32, name="kv")
             nc.tensor.matmul_mx(
                 out=kv[:].rearrange("p h s d -> p (h s d)"),
-                lhsT=c_codes[n, i][:].bitcast(FP8X4),
-                lhsT_scale=c_scales[n, i][:],
+                lhsT=c_codes[n][:, i].bitcast(FP8X4),
+                lhsT_scale=c_scales[n][:, i],
                 rhs=wb_codes[:].bitcast(FP8X4),
                 rhs_scale=wb_scales[:],
                 start=True,
@@ -312,9 +309,8 @@ def tile_multilatentattention_pb_t_kernel(tc, x, Wkva, Wkvb, out_0, out_1):
             if live(n + 1):
                 quantise_x(n + 1)
             if live(n):
-                quantise_latent(n, 0)
                 rope_products(n)
-                quantise_latent(n, 1)
+                quantise_latent(n)
             if live(n - 1):
                 expand(n - 1, 0)
                 expand(n - 1, 1)

@@ -67,11 +67,14 @@ def tile_multilatentattention_pb_t_kernel(tc, x, Wkva, Wkvb, out_0, out_1):
             nc.sync.dma_start(out=wa_raw[:, g].rearrange("q t c -> q (t c)"), in_=wa_rows[g])
         x_sb = {}
 
-        def load_x(n):
-            x_sb[n] = x_pool.tile([P, TILES * D], BF16, name="x_sb")
-            nc.sync.dma_start(out=x_sb[n][:], in_=x_units[n])
+        def load_x(n, first=0, last=TILES):
+            if first == 0:
+                x_sb[n] = x_pool.tile([P, TILES * D], BF16, name="x_sb")
+            cols = slice(first * D, last * D)
+            nc.sync.dma_start(out=x_sb[n][:, cols], in_=x_units[n][:, cols])
 
-        load_x(0)
+        for i in range(TILES):
+            load_x(0, i, i + 1)
         load_x(1)
         wb_raw = keep.tile([P, PACK, KV], BF16)
         nc.sync.dma_start(out=wb_raw[:], in_=Wkvb.rearrange("(q m) n -> q m n", q=P))
@@ -119,19 +122,21 @@ def tile_multilatentattention_pb_t_kernel(tc, x, Wkva, Wkvb, out_0, out_1):
         )
         frac = keep.tile(table_shape, F32)
         nc.vector.tensor_sub(out=frac[:], in0=angle[:], in1=whole[:])
-        sin_half = keep.tile(table_shape, F32)
         factors = keep.tile([P, PHASES * TILES, 2, 2, PAIRS], F32)
+        sin_half = keep.tile(table_shape, F32)
         nc.scalar.activation(out=factors[:, :, 1, 0, :], in_=frac[:], func=ACT.Sin, scale=2.0 * math.pi)
         nc.scalar.activation(out=factors[:, :, 1, 1, :], in_=frac[:], func=ACT.Sin, scale=-2.0 * math.pi)
         nc.scalar.activation(out=sin_half[:], in_=frac[:], func=ACT.Sin, scale=math.pi)
-        nc.scalar.activation(out=sin_half[:], in_=sin_half[:], func=ACT.Square)
-        nc.scalar.activation(
-            out=factors[:, :, 0, :, :],
-            in_=sin_half[:].unsqueeze(2).to_broadcast([P, PHASES * TILES, 2, PAIRS]),
-            func=ACT.Copy,
-            scale=-2.0,
-            bias=1.0,
-        )
+
+        def finish_factors():
+            nc.scalar.activation(out=sin_half[:], in_=sin_half[:], func=ACT.Square)
+            nc.scalar.activation(
+                out=factors[:, :, 0, :, :],
+                in_=sin_half[:].unsqueeze(2).to_broadcast([P, PHASES * TILES, 2, PAIRS]),
+                func=ACT.Copy,
+                scale=-2.0,
+                bias=1.0,
+            )
 
         def regroup(engine_copy, grouped, raw):
             engine_copy(
@@ -153,10 +158,6 @@ def tile_multilatentattention_pb_t_kernel(tc, x, Wkva, Wkvb, out_0, out_1):
             nc.vector.tensor_copy(
                 out=wa_grouped[:, g, latent_cols, :].rearrange("q (m j) t -> q m j t", m=PACK),
                 in_=wa_raw[:, g, :, latent_cols].rearrange("q t (j m) -> q m j t", m=PACK),
-            )
-            nc.scalar.copy(
-                out=wa_grouped[:, g, rope_cols, :].rearrange("q (e j) t -> q e j t", e=2),
-                in_=wa_raw[:, g, :, rope_cols].rearrange("q t (j e) -> q e j t", e=2),
             )
             quantise(
                 wa_codes[:, g, latent_cols], wa_scales[:, g, latent_cols], wa_grouped[:, g, latent_cols, :]
@@ -322,11 +323,33 @@ def tile_multilatentattention_pb_t_kernel(tc, x, Wkva, Wkvb, out_0, out_1):
 
         turn(-2)
         turn(-1)
+        finish_factors()
+        for g in range(PASSES):
+            nc.vector.tensor_copy(
+                out=wa_grouped[:, g, rope_cols, :].rearrange("q (e j) t -> q e j t", e=2),
+                in_=wa_raw[:, g, :, rope_cols].rearrange("q t (j e) -> q e j t", e=2),
+            )
+        quantise_x(1)
+        latent(0, 0)
+        latent(0, 1)
         for g in range(PASSES):
             quantise(wa_codes[:, g, rope_cols], wa_scales[:, g, rope_cols], wa_grouped[:, g, rope_cols, :])
+        rope_products(0)
+        transpose_unit(2)
+        quantise_latent(0)
         regroup(nc.vector.tensor_copy, wb_grouped[:, 0 : KV // 2, :], wb_raw[:, :, 0 : KV // 2])
         regroup(nc.scalar.copy, wb_grouped[:, KV // 2 : KV, :], wb_raw[:, :, KV // 2 : KV])
-        turn(0)
+        rope_finish(0)
+        latent(1, 0)
+        latent(1, 1)
         quantise(wb_codes[:], wb_scales[:], wb_grouped[:])
-        for n in range(1, UNITS + 1):
+        quantise_x(2)
+        rope_products(1)
+        quantise_latent(1)
+        transpose_unit(3)
+        expand(0, 0)
+        expand(0, 1)
+        store(0)
+        rope_finish(1)
+        for n in range(2, UNITS + 1):
             turn(n)

@@ -33,6 +33,8 @@ TILES = 2
 UNIT = TILES * P
 UNITS = TOKENS // UNIT
 PHASES = SEQ // UNIT
+BLOCK_UNITS = 2
+BLOCK_TILES = BLOCK_UNITS * TILES
 
 ROUND_MAGIC = 1.5 * 2.0**23
 
@@ -41,20 +43,20 @@ FLOPS = 2 * TOKENS * D * CKV + 2 * TOKENS * KL * KV
 
 def tile_multilatentattention_pb_t_kernel(tc, x, Wkva, Wkvb, out_0, out_1):
     nc = tc.nc
-    x_units = x.flatten_outer_dims().rearrange("(n p i) k -> n p (i k)", p=P, i=TILES)
-    kf_units = out_0.rearrange("b s h f -> (b s) (h f)").rearrange(
-        "(n p i) f -> n p (i f)", p=P, i=TILES
+    x_blocks = x.flatten_outer_dims().rearrange("(n p i) k -> n p (i k)", p=P, i=BLOCK_TILES)
+    kf_blocks = out_0.rearrange("b s h f -> (b s) (h f)").rearrange(
+        "(n p i) f -> n p (i f)", p=P, i=BLOCK_TILES
     )
-    v_units = out_1.rearrange("b s h f -> (b s) (h f)").rearrange(
-        "(n p i) f -> n p (i f)", p=P, i=TILES
+    v_blocks = out_1.rearrange("b s h f -> (b s) (h f)").rearrange(
+        "(n p i) f -> n p (i f)", p=P, i=BLOCK_TILES
     )
 
     with ExitStack() as ctx:
         keep = ctx.enter_context(tc.tile_pool(name="keep", bufs=1))
-        x_pool = ctx.enter_context(tc.tile_pool(name="x_pool", bufs=UNITS))
+        x_pool = ctx.enter_context(tc.tile_pool(name="x_pool", bufs=UNITS // BLOCK_UNITS))
         stage = ctx.enter_context(tc.tile_pool(name="stage", bufs=3))
         codes = ctx.enter_context(tc.tile_pool(name="codes", bufs=3))
-        results = ctx.enter_context(tc.tile_pool(name="results", bufs=8))
+        results = ctx.enter_context(tc.tile_pool(name="results", bufs=4))
         xt_banks = ctx.enter_context(tc.psum_pool(name="xt_banks", bufs=3))
         c_banks = ctx.enter_context(tc.psum_pool(name="c_banks", bufs=2))
         kv_banks = ctx.enter_context(tc.psum_pool(name="kv_banks", bufs=2))
@@ -67,26 +69,29 @@ def tile_multilatentattention_pb_t_kernel(tc, x, Wkva, Wkvb, out_0, out_1):
             nc.sync.dma_start(out=wa_raw[:, g].rearrange("q t c -> q (t c)"), in_=wa_rows[g])
         x_sb = {}
 
-        def load_x(n, first=0, last=TILES):
+        def load_x(b, first=0, last=BLOCK_TILES):
             if first == 0:
-                x_sb[n] = x_pool.tile([P, TILES * D], BF16, name="x_sb")
+                x_sb[b] = x_pool.tile([P, BLOCK_TILES * D], BF16, name="x_sb")
             cols = slice(first * D, last * D)
-            nc.sync.dma_start(out=x_sb[n][:, cols], in_=x_units[n][:, cols])
+            nc.sync.dma_start(out=x_sb[b][:, cols], in_=x_blocks[b][:, cols])
 
-        for i in range(TILES):
-            load_x(0, i, i + 1)
-        load_x(1)
+        load_x(0, 0, 1)
+        load_x(0, 1, 2)
+        load_x(0, 2, 4)
         wb_raw = keep.tile([P, PACK, KV], BF16)
         nc.sync.dma_start(out=wb_raw[:], in_=Wkvb.rearrange("(q m) n -> q m n", q=P))
-        for n in range(2, UNITS):
-            load_x(n)
+        for b in range(1, UNITS // BLOCK_UNITS):
+            load_x(b)
 
         warm = keep.tile([P, 1], F32)
         nc.vector.memset(warm[:], 0.0)
         nc.scalar.activation(out=warm[:], in_=warm[:], func=ACT.Sin)
         pos_i = keep.tile([P, PHASES * TILES], I32)
         nc.gpsimd.iota(
-            pos_i[:], pattern=[[UNIT, PHASES], [1, TILES]], base=0, channel_multiplier=TILES
+            pos_i[:],
+            pattern=[[BLOCK_UNITS * UNIT, PHASES // BLOCK_UNITS], [1, BLOCK_TILES]],
+            base=0,
+            channel_multiplier=BLOCK_TILES,
         )
         ident = keep.tile([P, P], F32)
         make_identity(nc, ident[:])
@@ -173,18 +178,21 @@ def tile_multilatentattention_pb_t_kernel(tc, x, Wkva, Wkvb, out_0, out_1):
         c_codes = {}
         c_scales = {}
         products = {}
+        kf_block = {}
+        v_block = {}
         kf_t = {}
         v_t = {}
         half = D // 2
 
         def transpose_unit(n):
             x_grouped[n] = stage.tile([P, TILES * D], BF16, name="x_grouped", align_bytes=64)
-            words_in = x_sb[n][:].bitcast(F32)
+            words_in = x_sb[n // BLOCK_UNITS][:].bitcast(F32)
+            first_tile = n % BLOCK_UNITS * TILES
             words_out = x_grouped[n][:].bitcast(F32)
             for i in range(TILES):
                 xt = xt_banks.tile([P, half], F32, name="xt")
                 for g in range(PASSES):
-                    first = i * half + g * 2 * P
+                    first = (first_tile + i) * half + g * 2 * P
                     for u in range(2):
                         nc.tensor.transpose(
                             xt[:, (2 * g + u) * P : (2 * g + u + 1) * P],
@@ -234,7 +242,12 @@ def tile_multilatentattention_pb_t_kernel(tc, x, Wkva, Wkvb, out_0, out_1):
             )
 
         def rope_finish(n):
-            kf_t[n] = results.tile([P, TILES, H, ND + RD], F32, name="kf_t")
+            if n % BLOCK_UNITS == 0:
+                kf_block[n] = results.tile([P, BLOCK_TILES, H, ND + RD], F32, name="kf_block")
+                v_block[n] = results.tile([P, BLOCK_TILES, H, VD], F32, name="v_block")
+            first_tile = n % BLOCK_UNITS * TILES
+            kf_t[n] = kf_block[n - n % BLOCK_UNITS][:, first_tile : first_tile + TILES]
+            v_t[n] = v_block[n - n % BLOCK_UNITS][:, first_tile : first_tile + TILES]
             halves = products[n][:].rearrange("p k i (e j) -> p k i j e", e=2)
             nc.vector.tensor_tensor(
                 out=kf_t[n][:, :, 0, ND:].rearrange("p i (j e) -> p i j e", e=2),
@@ -291,14 +304,22 @@ def tile_multilatentattention_pb_t_kernel(tc, x, Wkva, Wkvb, out_0, out_1):
                 start=True,
                 stop=True,
             )
-            if i == 0:
-                v_t[n] = results.tile([P, TILES, H, VD], F32, name="v_t")
             nc.scalar.copy(out=kf_t[n][:, i, :, 0:ND], in_=kv[:, :, 0, :])
             nc.scalar.copy(out=v_t[n][:, i, :, :], in_=kv[:, :, 1, :])
 
         def store(n):
-            nc.sync.dma_start(out=kf_units[n], in_=kf_t[n][:].rearrange("p i h f -> p (i h f)"))
-            nc.sync.dma_start(out=v_units[n], in_=v_t[n][:].rearrange("p i h f -> p (i h f)"))
+            b, u = divmod(n, BLOCK_UNITS)
+            if b >= UNITS // BLOCK_UNITS - 2:
+                tiles = slice(u * TILES, (u + 1) * TILES)
+            elif u == BLOCK_UNITS - 1:
+                tiles = slice(0, BLOCK_TILES)
+            else:
+                return
+            for blocks, sb, width in ((kf_blocks, kf_block, H * (ND + RD)), (v_blocks, v_block, H * VD)):
+                nc.sync.dma_start(
+                    out=blocks[b][:, tiles.start * width : tiles.stop * width],
+                    in_=sb[b * BLOCK_UNITS][:, tiles].rearrange("p i h f -> p (i h f)"),
+                )
 
         def live(n):
             return 0 <= n < UNITS

@@ -171,6 +171,7 @@ def tile_multilatentattention_pb_t_kernel(tc, x, Wkva, Wkvb, out_0, out_1):
         wb_codes = keep.tile([P, KV], U32, align_bytes=64)
         wb_scales = keep.tile([P, KV], U8, align_bytes=64)
 
+        x_split = {}
         x_grouped = {}
         x_codes = {}
         x_scales = {}
@@ -184,6 +185,16 @@ def tile_multilatentattention_pb_t_kernel(tc, x, Wkva, Wkvb, out_0, out_1):
         v_t = {}
         half = D // 2
 
+        def split_words(n, i):
+            x_split[n, i] = stage.tile([P, half], F32, name="x_split")
+            first = (n % BLOCK_UNITS * TILES + i) * half
+            nc.vector.tensor_copy(
+                out=x_split[n, i][:].rearrange("p (g u r) -> p g u r", g=PASSES, u=2),
+                in_=x_sb[n // BLOCK_UNITS][:]
+                .bitcast(F32)[:, first : first + half]
+                .rearrange("p (g r u) -> p g u r", g=PASSES, u=2),
+            )
+
         def transpose_unit(n):
             x_grouped[n] = stage.tile([P, TILES * D], BF16, name="x_grouped", align_bytes=64)
             words_in = x_sb[n // BLOCK_UNITS][:].bitcast(F32)
@@ -194,11 +205,12 @@ def tile_multilatentattention_pb_t_kernel(tc, x, Wkva, Wkvb, out_0, out_1):
                 for g in range(PASSES):
                     first = (first_tile + i) * half + g * 2 * P
                     for u in range(2):
-                        nc.tensor.transpose(
-                            xt[:, (2 * g + u) * P : (2 * g + u + 1) * P],
-                            words_in[:, first + u : first + 2 * P : 2],
-                            ident[:],
-                        )
+                        block = slice((2 * g + u) * P, (2 * g + u + 1) * P)
+                        if (n, i) in x_split:
+                            block_in = x_split[n, i][:, block]
+                        else:
+                            block_in = words_in[:, first + u : first + 2 * P : 2]
+                        nc.tensor.transpose(xt[:, block], block_in, ident[:])
                 nc.scalar.copy(
                     out=words_out[:, i * half : (i + 1) * half].rearrange(
                         "q (g r u) -> q g r u", g=PASSES, u=2
@@ -327,11 +339,13 @@ def tile_multilatentattention_pb_t_kernel(tc, x, Wkva, Wkvb, out_0, out_1):
         def turn(n):
             if live(n):
                 latent(n, 0)
+                rope_products(n)
                 latent(n, 1)
             if live(n + 1):
                 quantise_x(n + 1)
+            if live(n + 3):
+                split_words(n + 3, 1)
             if live(n):
-                rope_products(n)
                 quantise_latent(n)
             if live(n - 1):
                 expand(n - 1, 0)
@@ -342,8 +356,9 @@ def tile_multilatentattention_pb_t_kernel(tc, x, Wkva, Wkvb, out_0, out_1):
             if live(n):
                 rope_finish(n)
 
-        turn(-2)
-        turn(-1)
+        transpose_unit(0)
+        quantise_x(0)
+        transpose_unit(1)
         finish_factors()
         for g in range(PASSES):
             nc.vector.tensor_copy(

@@ -143,12 +143,6 @@ def tile_multilatentattention_pb_t_kernel(tc, x, Wkva, Wkvb, out_0, out_1):
                 bias=1.0,
             )
 
-        def regroup(engine_copy, grouped, raw):
-            engine_copy(
-                out=grouped.rearrange("q (c r) t -> q c t r", r=4),
-                in_=raw.rearrange("q t (c r) -> q c t r", r=4),
-            )
-
         def quantise(words, scales, grouped):
             nc.vector.quantize_mx(
                 out=words.bitcast(FP8X4), scales=scales, in_=grouped.rearrange("q c t -> q (c t)")
@@ -168,6 +162,8 @@ def tile_multilatentattention_pb_t_kernel(tc, x, Wkva, Wkvb, out_0, out_1):
                 wa_codes[:, g, latent_cols], wa_scales[:, g, latent_cols], wa_grouped[:, g, latent_cols, :]
             )
         wb_grouped = keep.tile([P, KV, PACK], BF16, align_bytes=64)
+        nope_cols = slice(0, H * ND)
+        v_cols = slice(H * ND, KV)
         wb_codes = keep.tile([P, KV], U32, align_bytes=64)
         wb_scales = keep.tile([P, KV], U8, align_bytes=64)
 
@@ -305,19 +301,24 @@ def tile_multilatentattention_pb_t_kernel(tc, x, Wkva, Wkvb, out_0, out_1):
                 in_=c_grouped[n][:].rearrange("q i r t -> q (i r t)"),
             )
 
-        def expand(n, i):
-            kv = kv_banks.tile([P, H, 2, ND], F32, name="kv")
-            nc.tensor.matmul_mx(
-                out=kv[:].rearrange("p h s d -> p (h s d)"),
-                lhsT=c_codes[n][:, i].bitcast(FP8X4),
-                lhsT_scale=c_scales[n][:, i],
-                rhs=wb_codes[:].bitcast(FP8X4),
-                rhs_scale=wb_scales[:],
-                start=True,
-                stop=True,
+        def expand(n):
+            kf_bank = kv_banks.tile([P, TILES, H * ND], F32, name="kv")
+            v_bank = kv_banks.tile([P, TILES, H * VD], F32, name="kv")
+            for bank, cols in ((kf_bank, nope_cols), (v_bank, v_cols)):
+                for i in range(TILES):
+                    nc.tensor.matmul_mx(
+                        out=bank[:, i],
+                        lhsT=c_codes[n][:, i].bitcast(FP8X4),
+                        lhsT_scale=c_scales[n][:, i],
+                        rhs=wb_codes[:, cols].bitcast(FP8X4),
+                        rhs_scale=wb_scales[:, cols],
+                        start=True,
+                        stop=True,
+                    )
+            nc.scalar.copy(
+                out=kf_t[n][:, :, :, 0:ND], in_=kf_bank[:].rearrange("p i (h d) -> p i h d", h=H)
             )
-            nc.scalar.copy(out=kf_t[n][:, i, :, 0:ND], in_=kv[:, :, 0, :])
-            nc.scalar.copy(out=v_t[n][:, i, :, :], in_=kv[:, :, 1, :])
+            nc.scalar.copy(out=v_t[n][:], in_=v_bank[:].rearrange("p i (h d) -> p i h d", h=H))
 
         def store(n):
             b, u = divmod(n, BLOCK_UNITS)
@@ -348,8 +349,7 @@ def tile_multilatentattention_pb_t_kernel(tc, x, Wkva, Wkvb, out_0, out_1):
             if live(n):
                 quantise_latent(n)
             if live(n - 1):
-                expand(n - 1, 0)
-                expand(n - 1, 1)
+                expand(n - 1)
                 store(n - 1)
             if live(n + 2):
                 transpose_unit(n + 2)
@@ -373,8 +373,13 @@ def tile_multilatentattention_pb_t_kernel(tc, x, Wkva, Wkvb, out_0, out_1):
         rope_products(0)
         transpose_unit(2)
         quantise_latent(0)
-        regroup(nc.vector.tensor_copy, wb_grouped[:, 0 : KV // 2, :], wb_raw[:, :, 0 : KV // 2])
-        regroup(nc.scalar.copy, wb_grouped[:, KV // 2 : KV, :], wb_raw[:, :, KV // 2 : KV])
+        wb_by_part = wb_raw[:].rearrange("q t (h s d) -> q s h d t", h=H, s=2)
+        nc.vector.tensor_copy(
+            out=wb_grouped[:, nope_cols, :].rearrange("q (h d) t -> q h d t", h=H), in_=wb_by_part[:, 0]
+        )
+        nc.scalar.copy(
+            out=wb_grouped[:, v_cols, :].rearrange("q (h d) t -> q h d t", h=H), in_=wb_by_part[:, 1]
+        )
         rope_finish(0)
         latent(1, 0)
         latent(1, 1)
@@ -383,8 +388,7 @@ def tile_multilatentattention_pb_t_kernel(tc, x, Wkva, Wkvb, out_0, out_1):
         rope_products(1)
         quantise_latent(1)
         transpose_unit(3)
-        expand(0, 0)
-        expand(0, 1)
+        expand(0)
         store(0)
         rope_finish(1)
         for n in range(2, UNITS + 1):

@@ -149,8 +149,8 @@ def tile_multilatentattention_pb_t_kernel(tc, x, Wkva, Wkvb, out_0, out_1):
             )
 
         wa_grouped = keep.tile([P, PASSES, CKV, PACK], BF16, align_bytes=64)
-        wa_codes = keep.tile([P, PASSES, CKV], U32, align_bytes=64)
-        wa_scales = keep.tile([P, PASSES, CKV], U8, align_bytes=64)
+        wa_codes = keep.tile([P, PASSES, CKV], U32, align_bytes=256)
+        wa_scales = keep.tile([P, PASSES, CKV], U8, align_bytes=256)
         latent_cols = slice(0, KL)
         rope_cols = slice(KL, CKV)
         for g in range(PASSES):
@@ -164,8 +164,8 @@ def tile_multilatentattention_pb_t_kernel(tc, x, Wkva, Wkvb, out_0, out_1):
         wb_grouped = keep.tile([P, KV, PACK], BF16, align_bytes=64)
         nope_cols = slice(0, H * ND)
         v_cols = slice(H * ND, KV)
-        wb_codes = keep.tile([P, KV], U32, align_bytes=64)
-        wb_scales = keep.tile([P, KV], U8, align_bytes=64)
+        wb_codes = keep.tile([P, KV], U32, align_bytes=256)
+        wb_scales = keep.tile([P, KV], U8, align_bytes=256)
 
         x_split = {}
         x_grouped = {}
@@ -215,8 +215,8 @@ def tile_multilatentattention_pb_t_kernel(tc, x, Wkva, Wkvb, out_0, out_1):
                 )
 
         def quantise_x(n):
-            x_codes[n] = codes.tile([P, TILES * PASSES * P], U32, name="x_codes", align_bytes=64)
-            x_scales[n] = codes.tile([P, TILES * PASSES * P], U8, name="x_scales", align_bytes=64)
+            x_codes[n] = codes.tile([P, TILES * PASSES * P], U32, name="x_codes", align_bytes=256)
+            x_scales[n] = codes.tile([P, TILES * PASSES * P], U8, name="x_scales", align_bytes=256)
             nc.vector.quantize_mx(
                 out=x_codes[n][:].bitcast(FP8X4), scales=x_scales[n][:], in_=x_grouped[n][:]
             )
@@ -293,8 +293,8 @@ def tile_multilatentattention_pb_t_kernel(tc, x, Wkva, Wkvb, out_0, out_1):
                 nc.scalar.copy(out=c_grouped[n][:, i], in_=cb[:].rearrange("q m r -> q r m"))
 
         def quantise_latent(n):
-            c_codes[n] = codes.tile([P, TILES, P], U32, name="c_codes", align_bytes=64)
-            c_scales[n] = codes.tile([P, TILES, P], U8, name="c_scales", align_bytes=64)
+            c_codes[n] = codes.tile([P, TILES, P], U32, name="c_codes", align_bytes=256)
+            c_scales[n] = codes.tile([P, TILES, P], U8, name="c_scales", align_bytes=256)
             nc.vector.quantize_mx(
                 out=c_codes[n][:].rearrange("q i r -> q (i r)").bitcast(FP8X4),
                 scales=c_scales[n][:].rearrange("q i r -> q (i r)"),

import math
from contextlib import ExitStack

import concourse.mybir as mybir
from concourse.masks import make_identity

F32 = mybir.dt.float32
BF16 = mybir.dt.bfloat16
I32 = mybir.dt.int32
U32 = mybir.dt.uint32
U8 = mybir.dt.uint8
FP8X4 = mybir.dt.float8_e4m3fn_x4
ALU = mybir.AluOpType
ACT = mybir.ActivationFunctionType

P = 128
PACK = 4
TOKENS = 4 * 1024
SEQ = 1024
D = 1024
PASSES = D // (P * PACK)
KL = 512
RD = 128
PAIRS = RD // 2
H = 4
ND = 64
VD = 64
CKV = KL + RD
KV = H * (ND + VD)
ROPE_BASE = 10000.0

TILES = 2
UNIT = TILES * P
UNITS = TOKENS // UNIT
PHASES = SEQ // UNIT
BLOCK_UNITS = 2
BLOCK_TILES = BLOCK_UNITS * TILES

ROUND_MAGIC = 1.5 * 2.0**23

FLOPS = 2 * TOKENS * D * CKV + 2 * TOKENS * KL * KV


def tile_multilatentattention_pb_t_kernel(tc, x, Wkva, Wkvb, out_0, out_1):
    nc = tc.nc
    x_blocks = x.flatten_outer_dims().rearrange("(n p i) k -> n p (i k)", p=P, i=BLOCK_TILES)
    kf_blocks = out_0.rearrange("b s h f -> (b s) (h f)").rearrange(
        "(n p i) f -> n p (i f)", p=P, i=BLOCK_TILES
    )
    v_blocks = out_1.rearrange("b s h f -> (b s) (h f)").rearrange(
        "(n p i) f -> n p (i f)", p=P, i=BLOCK_TILES
    )

    with ExitStack() as ctx:
        keep = ctx.enter_context(tc.tile_pool(name="keep", bufs=1))
        x_pool = ctx.enter_context(tc.tile_pool(name="x_pool", bufs=UNITS // BLOCK_UNITS))
        stage = ctx.enter_context(tc.tile_pool(name="stage", bufs=3))
        codes = ctx.enter_context(tc.tile_pool(name="codes", bufs=3))
        results = ctx.enter_context(tc.tile_pool(name="results", bufs=4))
        xt_banks = ctx.enter_context(tc.psum_pool(name="xt_banks", bufs=3))
        c_banks = ctx.enter_context(tc.psum_pool(name="c_banks", bufs=2))
        kv_banks = ctx.enter_context(tc.psum_pool(name="kv_banks", bufs=2))
        pe_banks = ctx.enter_context(tc.psum_pool(name="pe_banks", bufs=1))
        ctx.enter_context(tc.manual_schedule())

        wa_rows = Wkva.rearrange("(g q t) c -> g q (t c)", g=PASSES, q=P, t=PACK)
        wa_raw = keep.tile([P, PASSES, PACK, CKV], BF16)
        for g in range(PASSES):
            nc.sync.dma_start(out=wa_raw[:, g].rearrange("q t c -> q (t c)"), in_=wa_rows[g])
        x_sb = {}

        def load_x(b, first=0, last=BLOCK_TILES):
            if first == 0:
                x_sb[b] = x_pool.tile([P, BLOCK_TILES * D], BF16, name="x_sb")
            cols = slice(first * D, last * D)
            nc.sync.dma_start(out=x_sb[b][:, cols], in_=x_blocks[b][:, cols])

        load_x(0, 0, 1)
        load_x(0, 1, 2)
        load_x(0, 2, 4)
        wb_raw = keep.tile([P, PACK, KV], BF16)
        nc.sync.dma_start(out=wb_raw[:], in_=Wkvb.rearrange("(q m) n -> q m n", q=P))
        for b in range(1, UNITS // BLOCK_UNITS):
            load_x(b)

        warm = keep.tile([P, 1], F32)
        nc.vector.memset(warm[:], 0.0)
        nc.scalar.activation(out=warm[:], in_=warm[:], func=ACT.Sin)
        pos_i = keep.tile([P, PHASES * TILES], I32)
        nc.gpsimd.iota(
            pos_i[:],
            pattern=[[BLOCK_UNITS * UNIT, PHASES // BLOCK_UNITS], [1, BLOCK_TILES]],
            base=0,
            channel_multiplier=BLOCK_TILES,
        )
        ident = keep.tile([P, P], F32)
        make_identity(nc, ident[:])
        pos = keep.tile([P, PHASES * TILES], F32)
        nc.vector.tensor_copy(out=pos[:], in_=pos_i[:])
        turns = keep.tile([P, PAIRS], F32)
        nc.vector.memset(turns[:, 0:1], 1.0)
        nc.vector.tensor_scalar_mul(out=turns[:, 0:1], in0=turns[:, 0:1], scalar1=0.5 / math.pi)
        filled = 1
        while filled < PAIRS:
            nc.vector.tensor_scalar_mul(
                out=turns[:, filled : 2 * filled],
                in0=turns[:, 0:filled],
                scalar1=ROPE_BASE ** (-2.0 * filled / RD),
            )
            filled *= 2
        table_shape = [P, PHASES * TILES, PAIRS]
        angle = keep.tile(table_shape, F32)
        nc.vector.tensor_tensor(
            out=angle[:],
            in0=pos[:].unsqueeze(2).to_broadcast(table_shape),
            in1=turns[:].unsqueeze(1).to_broadcast(table_shape),
            op=ALU.mult,
        )
        whole = keep.tile(table_shape, F32)
        nc.vector.tensor_scalar(
            out=whole[:],
            in0=angle[:],
            scalar1=ROUND_MAGIC,
            scalar2=ROUND_MAGIC,
            op0=ALU.add,
            op1=ALU.subtract,
        )
        frac = keep.tile(table_shape, F32)
        nc.vector.tensor_sub(out=frac[:], in0=angle[:], in1=whole[:])
        factors = keep.tile([P, PHASES * TILES, 2, 2, PAIRS], F32)
        sin_half = keep.tile(table_shape, F32)
        nc.scalar.activation(out=factors[:, :, 1, 0, :], in_=frac[:], func=ACT.Sin, scale=2.0 * math.pi)
        nc.scalar.activation(out=factors[:, :, 1, 1, :], in_=frac[:], func=ACT.Sin, scale=-2.0 * math.pi)
        nc.scalar.activation(out=sin_half[:], in_=frac[:], func=ACT.Sin, scale=math.pi)

        def finish_factors():
            nc.scalar.activation(out=sin_half[:], in_=sin_half[:], func=ACT.Square)
            nc.scalar.activation(
                out=factors[:, :, 0, :, :],
                in_=sin_half[:].unsqueeze(2).to_broadcast([P, PHASES * TILES, 2, PAIRS]),
                func=ACT.Copy,
                scale=-2.0,
                bias=1.0,
            )

        def quantise(words, scales, grouped):
            nc.vector.quantize_mx(
                out=words.bitcast(FP8X4), scales=scales, in_=grouped.rearrange("q c t -> q (c t)")
            )

        wa_grouped = keep.tile([P, PASSES, CKV, PACK], BF16, align_bytes=64)
        wa_codes = keep.tile([P, PASSES, CKV], U32, align_bytes=256)
        wa_scales = keep.tile([P, PASSES, CKV], U8, align_bytes=256)
        latent_cols = slice(0, KL)
        rope_cols = slice(KL, CKV)
        for g in range(PASSES):
            nc.vector.tensor_copy(
                out=wa_grouped[:, g, latent_cols, :].rearrange("q (m j) t -> q m j t", m=PACK),
                in_=wa_raw[:, g, :, latent_cols].rearrange("q t (j m) -> q m j t", m=PACK),
            )
            quantise(
                wa_codes[:, g, latent_cols], wa_scales[:, g, latent_cols], wa_grouped[:, g, latent_cols, :]
            )
        wb_grouped = keep.tile([P, KV, PACK], BF16, align_bytes=64)
        nope_cols = slice(0, H * ND)
        v_cols = slice(H * ND, KV)
        wb_codes = keep.tile([P, KV], U32, align_bytes=256)
        wb_scales = keep.tile([P, KV], U8, align_bytes=256)

        x_split = {}
        x_grouped = {}
        x_codes = {}
        x_scales = {}
        c_grouped = {}
        c_codes = {}
        c_scales = {}
        products = {}
        kf_block = {}
        v_block = {}
        kf_t = {}
        v_t = {}
        half = D // 2

        def split_words(n, i):
            x_split[n, i] = stage.tile([P, half], F32, name="x_split")
            first = (n % BLOCK_UNITS * TILES + i) * half
            nc.vector.tensor_copy(
                out=x_split[n, i][:].rearrange("p (g u r) -> p g u r", g=PASSES, u=2),
                in_=x_sb[n // BLOCK_UNITS][:]
                .bitcast(F32)[:, first : first + half]
                .rearrange("p (g r u) -> p g u r", g=PASSES, u=2),
            )

        def transpose_unit(n):
            x_grouped[n] = stage.tile([P, TILES * D], BF16, name="x_grouped", align_bytes=64)
            words_in = x_sb[n // BLOCK_UNITS][:].bitcast(F32)
            first_tile = n % BLOCK_UNITS * TILES
            words_out = x_grouped[n][:].bitcast(F32)
            for i in range(TILES):
                xt = xt_banks.tile([P, half], F32, name="xt")
                for g in range(PASSES):
                    first = (first_tile + i) * half + g * 2 * P
                    for u in range(2):
                        block = slice((2 * g + u) * P, (2 * g + u + 1) * P)
                        if (n, i) in x_split:
                            block_in = x_split[n, i][:, block]
                        else:
                            block_in = words_in[:, first + u : first + 2 * P : 2]
                        nc.tensor.transpose(xt[:, block], block_in, ident[:])
                nc.scalar.copy(
                    out=words_out[:, i * half : (i + 1) * half].rearrange(
                        "q (g r u) -> q g r u", g=PASSES, u=2
                    ),
                    in_=xt[:].rearrange("q (g u r) -> q g r u", g=PASSES, u=2),
                )

        def quantise_x(n):
            x_codes[n] = codes.tile([P, TILES * PASSES * P], U32, name="x_codes", align_bytes=256)
            x_scales[n] = codes.tile([P, TILES * PASSES * P], U8, name="x_scales", align_bytes=256)
            nc.vector.quantize_mx(
                out=x_codes[n][:].bitcast(FP8X4), scales=x_scales[n][:], in_=x_grouped[n][:]
            )

        def x_cols(i, g):
            return slice((i * PASSES + g) * P, (i * PASSES + g + 1) * P)

        def rope_products(n):
            pe = pe_banks.tile([P, TILES, 2, PAIRS], F32, name="pe")
            for i in range(TILES):
                for g in range(PASSES):
                    nc.tensor.matmul_mx(
                        out=pe[:, i].rearrange("p e j -> p (e j)"),
                        lhsT=x_codes[n][:, x_cols(i, g)].bitcast(FP8X4),
                        lhsT_scale=x_scales[n][:, x_cols(i, g)],
                        rhs=wa_codes[:, g, rope_cols].bitcast(FP8X4),
                        rhs_scale=wa_scales[:, g, rope_cols],
                        start=(g == 0),
                        stop=(g == PASSES - 1),
                    )
            row = (n % PHASES) * TILES
            products[n] = stage.tile([P, 2, TILES, 2 * PAIRS], F32, name="products")
            nc.vector.tensor_tensor(
                out=products[n][:],
                in0=pe[:]
                .rearrange("p i e j -> p i (e j)")
                .unsqueeze(1)
                .to_broadcast([P, 2, TILES, 2 * PAIRS]),
                in1=factors[:, row : row + TILES].rearrange("p i k e j -> p k i (e j)"),
                op=ALU.mult,
            )

        def rope_finish(n):
            if n % BLOCK_UNITS == 0:
                kf_block[n] = results.tile([P, BLOCK_TILES, H, ND + RD], F32, name="kf_block")
                v_block[n] = results.tile([P, BLOCK_TILES, H, VD], F32, name="v_block")
            first_tile = n % BLOCK_UNITS * TILES
            kf_t[n] = kf_block[n - n % BLOCK_UNITS][:, first_tile : first_tile + TILES]
            v_t[n] = v_block[n - n % BLOCK_UNITS][:, first_tile : first_tile + TILES]
            halves = products[n][:].rearrange("p k i (e j) -> p k i j e", e=2)
            nc.vector.tensor_tensor(
                out=kf_t[n][:, :, 0, ND:].rearrange("p i (j e) -> p i j e", e=2),
                in0=halves[:, 0],
                in1=halves[:, 1, :, :, ::-1],
                op=ALU.add,
            )
            nc.gpsimd.tensor_scalar(
                out=kf_t[n][:, :, 1:H, ND:],
                in0=kf_t[n][:, :, 0:1, ND:].to_broadcast([P, TILES, H - 1, RD]),
                scalar1=1.0,
                scalar2=0.0,
                op0=ALU.mult,
                op1=ALU.add,
            )

        def latent(n, i):
            cb = c_banks.tile([P, PACK, P], F32, name="cb")
            for m in range(PACK):
                for g in range(PASSES):
                    nc.tensor.matmul_mx(
                        out=cb[:, m, :],
                        lhsT=wa_codes[:, g, m * P : (m + 1) * P].bitcast(FP8X4),
                        lhsT_scale=wa_scales[:, g, m * P : (m + 1) * P],
                        rhs=x_codes[n][:, x_cols(i, g)].bitcast(FP8X4),
                        rhs_scale=x_scales[n][:, x_cols(i, g)],
                        start=(g == 0),
                        stop=(g == PASSES - 1),
                    )
            if i == 0:
                c_grouped[n] = stage.tile([P, TILES, P, PACK], BF16, name="c_grouped", align_bytes=64)
            if i == 0:
                nc.vector.tensor_copy(out=c_grouped[n][:, i], in_=cb[:].rearrange("q m r -> q r m"))
            else:
                nc.scalar.copy(out=c_grouped[n][:, i], in_=cb[:].rearrange("q m r -> q r m"))

        def quantise_latent(n):
            c_codes[n] = codes.tile([P, TILES, P], U32, name="c_codes", align_bytes=256)
            c_scales[n] = codes.tile([P, TILES, P], U8, name="c_scales", align_bytes=256)
            nc.vector.quantize_mx(
                out=c_codes[n][:].rearrange("q i r -> q (i r)").bitcast(FP8X4),
                scales=c_scales[n][:].rearrange("q i r -> q (i r)"),
                in_=c_grouped[n][:].rearrange("q i r t -> q (i r t)"),
            )

        def expand(n):
            kf_bank = kv_banks.tile([P, TILES, H * ND], F32, name="kv")
            v_bank = kv_banks.tile([P, TILES, H * VD], F32, name="kv")
            for bank, cols in ((kf_bank, nope_cols), (v_bank, v_cols)):
                for i in range(TILES):
                    nc.tensor.matmul_mx(
                        out=bank[:, i],
                        lhsT=c_codes[n][:, i].bitcast(FP8X4),
                        lhsT_scale=c_scales[n][:, i],
                        rhs=wb_codes[:, cols].bitcast(FP8X4),
                        rhs_scale=wb_scales[:, cols],
                        start=True,
                        stop=True,
                    )
            nc.scalar.copy(
                out=kf_t[n][:, :, :, 0:ND], in_=kf_bank[:].rearrange("p i (h d) -> p i h d", h=H)
            )
            nc.scalar.copy(out=v_t[n][:], in_=v_bank[:].rearrange("p i (h d) -> p i h d", h=H))

        def store(n):
            b, u = divmod(n, BLOCK_UNITS)
            if b >= UNITS // BLOCK_UNITS - 2:
                tiles = slice(u * TILES, (u + 1) * TILES)
            elif u == BLOCK_UNITS - 1:
                tiles = slice(0, BLOCK_TILES)
            else:
                return
            for blocks, sb, width in ((kf_blocks, kf_block, H * (ND + RD)), (v_blocks, v_block, H * VD)):
                nc.sync.dma_start(
                    out=blocks[b][:, tiles.start * width : tiles.stop * width],
                    in_=sb[b * BLOCK_UNITS][:, tiles].rearrange("p i h f -> p (i h f)"),
                )

        def live(n):
            return 0 <= n < UNITS

        def turn(n):
            if live(n):
                latent(n, 0)
                rope_products(n)
                latent(n, 1)
            if live(n + 1):
                quantise_x(n + 1)
            if live(n + 3):
                split_words(n + 3, 1)
            if live(n):
                quantise_latent(n)
            if live(n - 1):
                expand(n - 1)
                store(n - 1)
            if live(n + 2):
                transpose_unit(n + 2)
            if live(n):
                rope_finish(n)

        transpose_unit(0)
        quantise_x(0)
        transpose_unit(1)
        finish_factors()
        for g in range(PASSES):
            nc.vector.tensor_copy(
                out=wa_grouped[:, g, rope_cols, :].rearrange("q (e j) t -> q e j t", e=2),
                in_=wa_raw[:, g, :, rope_cols].rearrange("q t (j e) -> q e j t", e=2),
            )
        quantise_x(1)
        latent(0, 0)
        latent(0, 1)
        for g in range(PASSES):
            quantise(wa_codes[:, g, rope_cols], wa_scales[:, g, rope_cols], wa_grouped[:, g, rope_cols, :])
        rope_products(0)
        transpose_unit(2)
        quantise_latent(0)
        wb_by_part = wb_raw[:].rearrange("q t (h s d) -> q s h d t", h=H, s=2)
        nc.vector.tensor_copy(
            out=wb_grouped[:, nope_cols, :].rearrange("q (h d) t -> q h d t", h=H), in_=wb_by_part[:, 0]
        )
        nc.scalar.copy(
            out=wb_grouped[:, v_cols, :].rearrange("q (h d) t -> q h d t", h=H), in_=wb_by_part[:, 1]
        )
        rope_finish(0)
        latent(1, 0)
        latent(1, 1)
        quantise(wb_codes[:], wb_scales[:], wb_grouped[:])
        quantise_x(2)
        rope_products(1)
        quantise_latent(1)
        transpose_unit(3)
        expand(0)
        store(0)
        rope_finish(1)
        for n in range(2, UNITS + 1):
            turn(n)
